import numpy as np
import ml_dtypes


def mxq(x, axis, fmt="e4m3"):
    dtype, down = {"e4m3": (ml_dtypes.float8_e4m3fn, 7), "e5m2": (ml_dtypes.float8_e5m2, 14)}[fmt]
    v = np.moveaxis(np.asarray(x, np.float32).astype(ml_dtypes.bfloat16).astype(np.float64), axis, -1)
    blocks = v.reshape(v.shape[:-1] + (-1, 32))
    amax = np.abs(blocks).max(-1, keepdims=True)
    byte = np.maximum(np.where(amax > 0, np.frexp(amax)[1] - 1 + 127, 0) - down, 1)
    scale = np.exp2(byte - 127.0)
    codes = (blocks / scale).astype(np.float32).astype(dtype).astype(np.float64)
    return np.moveaxis((codes * scale).reshape(v.shape), -1, axis)


WIDE = False


def mx_kscale(k):
    if not WIDE:
        return np.ones(k)
    levels = np.array([10, -10, 5, -5, 0])
    if k % 512:
        return np.exp2(np.random.permutation(np.resize(levels, k // 32))).repeat(32)
    a = np.empty((k // 512, 16))
    for p in range(k // 512):
        a[p, :8] = np.random.permutation(np.resize(levels, 8))
        for g in range(8):
            far = levels[np.abs(levels - a[p, g]) >= 10]
            a[p, g + 8] = far[np.random.randint(len(far))]
    return np.exp2(a.ravel()).repeat(32)


BF16 = ml_dtypes.bfloat16


def bf(x):
    return np.asarray(x, np.float32).astype(BF16)


def f64(x):
    return np.asarray(x).astype(np.float64)


T, D, F, R = 512, 1024, 2560, 128


def setup_inputs():
    s = mx_kscale(F)
    return {
        "h": bf(np.random.standard_normal((T, F)) * 0.75 * s),
        "ha": bf(np.random.standard_normal((T, R)) * 0.75),
        "W_down": bf(np.random.standard_normal((F, D)) / np.sqrt(F) / s[:, None]),
        "B_down": bf(np.random.standard_normal((R, D)) * 0.5 / np.sqrt(R)),
    }


def core(h, ha, W_down, B_down):
    return (mxq(f64(h), 1, "e4m3") @ mxq(f64(W_down), 0, "e4m3")) + f64(ha) @ f64(B_down)


def e4m3fn_bytes(y):
    return np.clip(np.asarray(y, np.float64), -448.0, 448.0).astype(np.float32).astype(ml_dtypes.float8_e4m3fn).view(np.uint8)


def reference(h, ha, W_down, B_down):
    out = core(h, ha, W_down, B_down)
    s = np.max(np.abs(out)) / 448.0
    return out, e4m3fn_bytes(out / s)

@@ -1,0 +1,259 @@
+from contextlib import ExitStack
+
+import concourse.mybir as mybir
+from concourse.masks import make_identity
+
+T, D, F, R = 512, 1024, 2560, 128
+FLOPS = 2 * T * F * D + 2 * T * R * D
+
+F32 = mybir.dt.float32
+BF16 = mybir.dt.bfloat16
+U32 = mybir.dt.uint32
+U8 = mybir.dt.uint8
+FP8X4 = mybir.dt.float8_e4m3fn_x4
+FP8 = mybir.dt.float8_e4m3fn
+ALU = mybir.AluOpType
+ACT = mybir.ActivationFunctionType
+AX = mybir.AxisListType
+
+P = 128
+PASSES = F // 512
+NH = 512
+H_LOADS = [(0, 1), (1, 3), (3, 5)]
+GROUPS = [(0, 512), (512, 256), (768, 256)]
+V_COLS = [256, 32, 0]
+V_COLS_LAST = 64
+FAST = False
+EPI = {7: [(0, 0)], 8: [(0, 1)], 9: [(0, 2)], 10: [(0, 3)], 12: [(1, 0), (1, 1)], 13: [(1, 2), (1, 3)]}
+S_FROM = 2688
+
+
+def tile_loramlp_pb_kernel(tc, h, ha, W_down, B_down, out_0, out_1):
+    nc = tc.nc
+    with ExitStack() as ctx:
+        keep = ctx.enter_context(tc.tile_pool(name="keep", bufs=1))
+        grp = ctx.enter_context(tc.tile_pool(name="grp", bufs=4))
+        psum = ctx.enter_context(tc.psum_pool(name="psum", bufs=8))
+        ctx.enter_context(tc.manual_schedule())
+
+        ha_sb = keep.tile([P, 4, R], BF16, name="ha_sb")
+        nc.sync.dma_start(out=ha_sb[:], in_=ha.rearrange("(p j) r -> p j r", j=4))
+        b_sb = keep.tile([P, D], BF16, name="b_sb")
+        h_of = {}
+        for n, (g0, g1) in enumerate(H_LOADS):
+            t = keep.tile([P, 4, 512 * (g1 - g0)], BF16, name="h_sb%d" % n)
+            nc.sync.dma_start(
+                out=t[:], in_=h[:, 512 * g0 : 512 * g1].rearrange("(p j) k -> p j k", j=4)
+            )
+            for g in range(g0, g1):
+                h_of[g] = (t, 512 * (g - g0))
+            if n == 0:
+                nc.sync.dma_start(out=b_sb[:], in_=B_down)
+        w_raw = {}
+        for half in range(2):
+            for g in range(PASSES):
+                t = keep.tile([P, 4, NH], BF16, name="w_raw%d_%d" % (half, g))
+                nc.sync.dma_start(
+                    out=t[:],
+                    in_=W_down[512 * g : 512 * (g + 1), NH * half : NH * (half + 1)].rearrange(
+                        "(p j) w -> p j w", j=4
+                    ),
+                )
+                w_raw[(half, g)] = t
+
+        ident_b = keep.tile([P, P], BF16, name="ident_b")
+        make_identity(nc, ident_b[:])
+        ident_f = keep.tile([P, P], F32, name="ident_f")
+        make_identity(nc, ident_f[:])
+        warm = keep.tile([P, 2], F32, name="warm")
+        nc.vector.memset(warm[:, 0:1], 0.0)
+        nc.scalar.activation(out=warm[:, 1:2], in_=warm[:, 0:1], func=ACT.Copy)
+
+        haT = keep.tile([P, 4, P], BF16, name="haT")
+        lora_sb = keep.tile([P, 4, D], F32, name="lora_sb")
+        out_sb = keep.tile([P, 4, D], F32, name="out_sb")
+        y_sb = keep.tile([P, 4 * D], F32, name="y_sb")
+        h_codes = keep.tile([P, PASSES, 512], U32, name="h_codes", align_bytes=64)
+        h_scales = keep.tile([P, PASSES, 512], U8, name="h_scales", align_bytes=64)
+        w_codes = keep.tile([P, PASSES, D], U32, name="w_codes", align_bytes=64)
+        w_scales = keep.tile([P, PASSES, D], U8, name="w_scales", align_bytes=64)
+        part = keep.tile([P, 12], F32, name="part")
+        stat = keep.tile([P, 4], F32, name="stat")
+        out0_v = out_0.rearrange("(p j) n -> p j n", j=4)
+        out1_v = out_1.rearrange("(p j) n -> p j n", j=4)
+
+        haT_ps = psum.tile([P, 4, P], BF16, tag="bank", name="haT_ps")
+        for j in range(4):
+            nc.tensor.transpose(haT_ps[:, j, :], ha_sb[:, j, :], ident_b[:])
+        nc.scalar.copy(out=haT[:], in_=haT_ps[:])
+
+        def lora(l):
+            half, j = l // 4, l % 4
+            cols = slice(NH * half, NH * (half + 1))
+            lp = psum.tile([P, NH], F32, tag="bank", name="lora_ps")
+            nc.tensor.matmul(lp[:], lhsT=haT[:, j, :], rhs=b_sb[:, cols], start=True, stop=True)
+            nc.scalar.copy(out=lora_sb[:, j, cols], in_=lp[:])
+
+        hg = []
+
+        def quant_h(g):
+            nc.vector.quantize_mx(
+                out=h_codes[:, g, :].bitcast(FP8X4), scales=h_scales[:, g, :], in_=hg[g][:]
+            )
+
+        for g in range(PASSES):
+            t = keep.tile([P, 2048], BF16, name="hg%d" % g, align_bytes=64)
+            hg.append(t)
+            t32 = t[:].bitcast(F32).rearrange("p (c u) -> p c u", u=2)
+            h_t, k0 = h_of[g]
+            for b in range(2):
+                xt = psum.tile([P, 2, 256], F32, tag="bank", name="xt")
+                for jj in range(2):
+                    words = h_t[:, 2 * b + jj, k0 : k0 + 512].bitcast(F32)
+                    for u in range(2):
+                        nc.tensor.transpose(
+                            xt[:, u, P * jj : P * (jj + 1)], words[:, u:256:2], ident_f[:]
+                        )
+                dst = t32[:, 256 * b : 256 * (b + 1), :]
+                src = xt[:].rearrange("p u r -> p r u")
+                if b == 0:
+                    nc.vector.tensor_copy(out=dst, in_=src)
+                else:
+                    nc.scalar.copy(out=dst, in_=src)
+            if g > 0:
+                quant_h(g - 1)
+            for l in (2 * g, 2 * g + 1):
+                if l < 8:
+                    lora(l)
+
+        chunks = [(q, g) for q in range(3) for g in range(PASSES)]
+        acc = {}
+        wgs = {}
+
+        def views(dst, src, lo, hi):
+            if FAST:
+                return (
+                    dst[:, lo:hi, :].rearrange("p (c i) t -> p c t i", i=4),
+                    src[:, :, lo:hi].rearrange("p t (c i) -> p c t i", i=4),
+                )
+            return dst[:, lo:hi, :], src[:, :, lo:hi].rearrange("p t w -> p w t")
+
+        def interleave(i):
+            q, g = chunks[i]
+            c0, w = GROUPS[q]
+            a = V_COLS_LAST if i == len(chunks) - 1 else V_COLS[q]
+            wg = grp.tile([P, w, 4], BF16, tag="wg", name="wg", align_bytes=64)
+            wgs[i] = wg
+            src = w_raw[(c0 // NH, g)][:, :, c0 % NH : c0 % NH + w]
+            if a > 0:
+                d, s = views(wg, src, 0, a)
+                nc.vector.tensor_copy(out=d, in_=s)
+            d, s = views(wg, src, a, w)
+            nc.scalar.copy(out=d, in_=s)
+
+        def quant_mm(i):
+            q, g = chunks[i]
+            c0, w = GROUPS[q]
+            cols = slice(c0, c0 + w)
+            nc.vector.quantize_mx(
+                out=w_codes[:, g, cols].bitcast(FP8X4),
+                scales=w_scales[:, g, cols],
+                in_=wgs[i][:].rearrange("p w j -> p (w j)"),
+            )
+            for j in range(4):
+                if g == 0:
+                    acc[(q, j)] = psum.tile([P, w], F32, tag="bank", name="acc%d%d" % (q, j))
+                tok = slice(P * j, P * (j + 1))
+                nc.tensor.matmul_mx(
+                    out=acc[(q, j)][:],
+                    lhsT=h_codes[:, g, tok].bitcast(FP8X4),
+                    lhsT_scale=h_scales[:, g, tok],
+                    rhs=w_codes[:, g, cols].bitcast(FP8X4),
+                    rhs_scale=w_scales[:, g, cols],
+                    start=(g == 0),
+                    stop=(g == PASSES - 1),
+                )
+
+        def add(q, j):
+            c0, w = GROUPS[q]
+            cols = slice(c0, c0 + w)
+            nc.vector.tensor_tensor(
+                out=out_sb[:, j, cols], in0=acc[(q, j)][:], in1=lora_sb[:, j, cols], op=ALU.add
+            )
+            nc.sync.dma_start(out=out0_v[:, j, cols], in_=out_sb[:, j, cols])
+
+        def red(q, j):
+            c0, w = GROUPS[q]
+            l = 4 * q + j
+            nc.vector.tensor_reduce(
+                out=part[:, l : l + 1],
+                in_=out_sb[:, j, c0 : c0 + w],
+                axis=AX.X,
+                op=ALU.max,
+                apply_absolute_value=True,
+            )
+
+        interleave(0)
+        quant_h(PASSES - 1)
+        for i in range(1, len(chunks)):
+            interleave(i)
+            for q, j in EPI.get(i, []):
+                add(q, j)
+            quant_mm(i - 1)
+            for q, j in EPI.get(i, []):
+                red(q, j)
+        quant_mm(len(chunks) - 1)
+        add(2, 0)
+        add(2, 1)
+        red(2, 0)
+        add(2, 2)
+        red(2, 1)
+        add(2, 3)
+        red(2, 2)
+        red(2, 3)
+
+        nc.vector.tensor_reduce(out=stat[:, 0:1], in_=part[:], axis=AX.X, op=ALU.max)
+        am_ps = psum.tile([P, P], F32, tag="bank", name="am_ps")
+        nc.tensor.transpose(am_ps[:], stat[:, 0:1].to_broadcast([P, P]), ident_f[:])
+        nc.vector.tensor_reduce(out=stat[:, 1:2], in_=am_ps[:], axis=AX.X, op=ALU.max)
+        nc.vector.reciprocal(out=stat[:, 2:3], in_=stat[:, 1:2])
+        rcp = stat[:, 2:3]
+
+        o_flat = out_sb[:].rearrange("p j n -> p (j n)")
+        f8 = [keep.tile([P, D], FP8, name="f8_%d" % j) for j in range(4)]
+
+        def v_mul(a, b):
+            nc.vector.tensor_scalar(
+                out=y_sb[:, a:b], in0=o_flat[:, a:b], scalar1=rcp, scalar2=448.0, op0=ALU.mult, op1=ALU.mult
+            )
+
+        def s_mul(a, b):
+            nc.scalar.activation(out=y_sb[:, a:b], in_=o_flat[:, a:b], func=ACT.Copy, scale=rcp)
+
+        def v_cast(a, b):
+            j = a // D
+            nc.vector.tensor_copy(out=f8[j][:, a - D * j : b - D * j], in_=y_sb[:, a:b], saturate=False)
+
+        def s_cast(a, b):
+            j = a // D
+            nc.scalar.activation(
+                out=f8[j][:, a - D * j : b - D * j], in_=y_sb[:, a:b], func=ACT.Copy, scale=448.0, saturate=False
+            )
+
+        def store(j):
+            nc.sync.dma_start(out=out1_v[:, j, :], in_=f8[j][:].bitcast(U8))
+
+        s_mul(3 * D, 4 * D)
+        v_mul(0, D)
+        v_mul(D, 2 * D)
+        v_cast(0, D)
+        store(0)
+        s_mul(S_FROM, 3 * D)
+        v_mul(2 * D, S_FROM)
+        v_cast(D, 2 * D)
+        store(1)
+        s_cast(3 * D, 4 * D)
+        store(3)
+        v_cast(2 * D, S_FROM)
+        s_cast(S_FROM, 3 * D)
+        store(2)

@@ -23,7 +23,7 @@ H_LOADS = [(0, 1), (1, 3), (3, 5)]
 GROUPS = [(0, 512), (512, 256), (768, 256)]
 V_COLS = [256, 32, 0]
 V_COLS_LAST = 64
-FAST = False
+FAST = True
 EPI = {7: [(0, 0)], 8: [(0, 1)], 9: [(0, 2)], 10: [(0, 3)], 12: [(1, 0), (1, 1)], 13: [(1, 2), (1, 3)]}
 S_FROM = 2688
 

@@ -19,12 +19,11 @@ AX = mybir.AxisListType
 P = 128
 PASSES = F // 512
 NH = 512
-H_LOADS = [(0, 1), (1, 3), (3, 5)]
+H_LOADS = [(0, 1), (1, 2), (2, 3), (3, 4), (4, 5)]
 GROUPS = [(0, 512), (512, 256), (768, 256)]
-V_COLS = [256, 32, 0]
-V_COLS_LAST = 64
-FAST = True
-EPI = {7: [(0, 0)], 8: [(0, 1)], 9: [(0, 2)], 10: [(0, 3)], 12: [(1, 0), (1, 1)], 13: [(1, 2), (1, 3)]}
+V_COLS = [288, 256, 256, 256, 256, 64, 32, 0, 0, 64, 0, 0, 0, 0, 64]
+FAST = False
+EPI = {7: [(0, 0)], 8: [(0, 1)], 9: [(0, 2)], 10: [(0, 3)], 11: [(1, 0)], 12: [(1, 1)], 13: [(1, 2)], 14: [(1, 3)]}
 S_FROM = 2688
 
 
@@ -141,7 +140,7 @@ def tile_loramlp_pb_kernel(tc, h, ha, W_down, B_down, out_0, out_1):
         def interleave(i):
             q, g = chunks[i]
             c0, w = GROUPS[q]
-            a = V_COLS_LAST if i == len(chunks) - 1 else V_COLS[q]
+            a = V_COLS[i]
             wg = grp.tile([P, w, 4], BF16, tag="wg", name="wg", align_bytes=64)
             wgs[i] = wg
             src = w_raw[(c0 // NH, g)][:, :, c0 % NH : c0 % NH + w]

@@ -19,11 +19,9 @@ AX = mybir.AxisListType
 P = 128
 PASSES = F // 512
 NH = 512
-H_LOADS = [(0, 1), (1, 2), (2, 3), (3, 4), (4, 5)]
-GROUPS = [(0, 512), (512, 256), (768, 256)]
-V_COLS = [288, 256, 256, 256, 256, 64, 32, 0, 0, 64, 0, 0, 0, 0, 64]
-FAST = False
-EPI = {7: [(0, 0)], 8: [(0, 1)], 9: [(0, 2)], 10: [(0, 3)], 11: [(1, 0)], 12: [(1, 1)], 13: [(1, 2)], 14: [(1, 3)]}
+H_LOADS = [(0, 1), (1, 3), (3, 5)]
+V_COLS = [256,256,256,256,256,256,256,256,256,256]
+POOL_TILES = [(0, 1), (0, 3), (1, 1), (1, 3)]
 S_FROM = 2688
 
 
@@ -48,17 +46,13 @@ def tile_loramlp_pb_kernel(tc, h, ha, W_down, B_down, out_0, out_1):
                 h_of[g] = (t, 512 * (g - g0))
             if n == 0:
                 nc.sync.dma_start(out=b_sb[:], in_=B_down)
-        w_raw = {}
-        for half in range(2):
-            for g in range(PASSES):
-                t = keep.tile([P, 4, NH], BF16, name="w_raw%d_%d" % (half, g))
-                nc.sync.dma_start(
-                    out=t[:],
-                    in_=W_down[512 * g : 512 * (g + 1), NH * half : NH * (half + 1)].rearrange(
-                        "(p j) w -> p j w", j=4
-                    ),
-                )
-                w_raw[(half, g)] = t
+        w_raw = []
+        for g in range(PASSES):
+            t = keep.tile([P, 4, D], BF16, name="w_raw%d" % g)
+            nc.sync.dma_start(
+                out=t[:], in_=W_down[512 * g : 512 * (g + 1), :].rearrange("(p j) w -> p j w", j=4)
+            )
+            w_raw.append(t)
 
         ident_b = keep.tile([P, P], BF16, name="ident_b")
         make_identity(nc, ident_b[:])
@@ -76,7 +70,7 @@ def tile_loramlp_pb_kernel(tc, h, ha, W_down, B_down, out_0, out_1):
         h_scales = keep.tile([P, PASSES, 512], U8, name="h_scales", align_bytes=64)
         w_codes = keep.tile([P, PASSES, D], U32, name="w_codes", align_bytes=64)
         w_scales = keep.tile([P, PASSES, D], U8, name="w_scales", align_bytes=64)
-        part = keep.tile([P, 12], F32, name="part")
+        part = keep.tile([P, 8], F32, name="part")
         stat = keep.tile([P, 4], F32, name="stat")
         out0_v = out_0.rearrange("(p j) n -> p j n", j=4)
         out1_v = out_1.rearrange("(p j) n -> p j n", j=4)
@@ -125,35 +119,22 @@ def tile_loramlp_pb_kernel(tc, h, ha, W_down, B_down, out_0, out_1):
                 if l < 8:
                     lora(l)
 
-        chunks = [(q, g) for q in range(3) for g in range(PASSES)]
+        chunks = [(g, half) for g in range(PASSES) for half in range(2)]
         acc = {}
         wgs = {}
 
-        def views(dst, src, lo, hi):
-            if FAST:
-                return (
-                    dst[:, lo:hi, :].rearrange("p (c i) t -> p c t i", i=4),
-                    src[:, :, lo:hi].rearrange("p t (c i) -> p c t i", i=4),
-                )
-            return dst[:, lo:hi, :], src[:, :, lo:hi].rearrange("p t w -> p w t")
-
         def interleave(i):
-            q, g = chunks[i]
-            c0, w = GROUPS[q]
+            g, half = chunks[i]
             a = V_COLS[i]
-            wg = grp.tile([P, w, 4], BF16, tag="wg", name="wg", align_bytes=64)
+            wg = grp.tile([P, NH, 4], BF16, tag="wg", name="wg", align_bytes=64)
             wgs[i] = wg
-            src = w_raw[(c0 // NH, g)][:, :, c0 % NH : c0 % NH + w]
-            if a > 0:
-                d, s = views(wg, src, 0, a)
-                nc.vector.tensor_copy(out=d, in_=s)
-            d, s = views(wg, src, a, w)
-            nc.scalar.copy(out=d, in_=s)
+            src = w_raw[g][:, :, NH * half : NH * (half + 1)].rearrange("p t w -> p w t")
+            nc.vector.tensor_copy(out=wg[:, 0:a, :], in_=src[:, 0:a, :])
+            nc.scalar.copy(out=wg[:, a:NH, :], in_=src[:, a:NH, :])
 
         def quant_mm(i):
-            q, g = chunks[i]
-            c0, w = GROUPS[q]
-            cols = slice(c0, c0 + w)
+            g, half = chunks[i]
+            cols = slice(NH * half, NH * (half + 1))
             nc.vector.quantize_mx(
                 out=w_codes[:, g, cols].bitcast(FP8X4),
                 scales=w_scales[:, g, cols],
@@ -161,10 +142,10 @@ def tile_loramlp_pb_kernel(tc, h, ha, W_down, B_down, out_0, out_1):
             )
             for j in range(4):
                 if g == 0:
-                    acc[(q, j)] = psum.tile([P, w], F32, tag="bank", name="acc%d%d" % (q, j))
+                    acc[(half, j)] = psum.tile([P, NH], F32, tag="bank", name="acc%d%d" % (half, j))
                 tok = slice(P * j, P * (j + 1))
                 nc.tensor.matmul_mx(
-                    out=acc[(q, j)][:],
+                    out=acc[(half, j)][:],
                     lhsT=h_codes[:, g, tok].bitcast(FP8X4),
                     lhsT_scale=h_scales[:, g, tok],
                     rhs=w_codes[:, g, cols].bitcast(FP8X4),
@@ -173,43 +154,50 @@ def tile_loramlp_pb_kernel(tc, h, ha, W_down, B_down, out_0, out_1):
                     stop=(g == PASSES - 1),
                 )
 
-        def add(q, j):
-            c0, w = GROUPS[q]
-            cols = slice(c0, c0 + w)
-            nc.vector.tensor_tensor(
-                out=out_sb[:, j, cols], in0=acc[(q, j)][:], in1=lora_sb[:, j, cols], op=ALU.add
-            )
-            nc.sync.dma_start(out=out0_v[:, j, cols], in_=out_sb[:, j, cols])
-
-        def red(q, j):
-            c0, w = GROUPS[q]
-            l = 4 * q + j
-            nc.vector.tensor_reduce(
-                out=part[:, l : l + 1],
-                in_=out_sb[:, j, c0 : c0 + w],
-                axis=AX.X,
-                op=ALU.max,
-                apply_absolute_value=True,
-            )
-
         interleave(0)
         quant_h(PASSES - 1)
         for i in range(1, len(chunks)):
             interleave(i)
-            for q, j in EPI.get(i, []):
-                add(q, j)
             quant_mm(i - 1)
-            for q, j in EPI.get(i, []):
-                red(q, j)
         quant_mm(len(chunks) - 1)
-        add(2, 0)
-        add(2, 1)
-        red(2, 0)
-        add(2, 2)
-        red(2, 1)
-        add(2, 3)
-        red(2, 2)
-        red(2, 3)
+
+        def tile_of(half, j):
+            return out_sb[:, j, NH * half : NH * (half + 1)], lora_sb[:, j, NH * half : NH * (half + 1)]
+
+        def store0(half, j):
+            o, lo = tile_of(half, j)
+            nc.sync.dma_start(out=out0_v[:, j, NH * half : NH * (half + 1)], in_=o)
+
+        def pool_add(half, j):
+            o, lo = tile_of(half, j)
+            mx = keep.tile([P, NH], F32, name="mx%d%d" % (half, j))
+            nc.scalar.copy(out=mx[:], in_=acc[(half, j)][:])
+            nc.gpsimd.tensor_tensor(out=o, in0=mx[:], in1=lo, op=ALU.add)
+
+        def add(half, j):
+            o, lo = tile_of(half, j)
+            nc.vector.tensor_tensor(out=o, in0=acc[(half, j)][:], in1=lo, op=ALU.add)
+            store0(half, j)
+
+        def red(half, j):
+            o, lo = tile_of(half, j)
+            l = 4 * half + j
+            nc.vector.tensor_reduce(
+                out=part[:, l : l + 1], in_=o, axis=AX.X, op=ALU.max, apply_absolute_value=True
+            )
+
+        tiles = [(half, j) for half in range(2) for j in range(4)]
+        for t in POOL_TILES:
+            pool_add(t[0], t[1])
+        mine = [t for t in tiles if t not in POOL_TILES]
+        add(mine[0][0], mine[0][1])
+        for n in range(1, len(mine)):
+            add(mine[n][0], mine[n][1])
+            red(mine[n - 1][0], mine[n - 1][1])
+        red(mine[-1][0], mine[-1][1])
+        for t in POOL_TILES:
+            store0(t[0], t[1])
+            red(t[0], t[1])
 
         nc.vector.tensor_reduce(out=stat[:, 0:1], in_=part[:], axis=AX.X, op=ALU.max)
         am_ps = psum.tile([P, P], F32, tag="bank", name="am_ps")

@@ -19,7 +19,6 @@ AX = mybir.AxisListType
 P = 128
 PASSES = F // 512
 NH = 512
-H_LOADS = [(0, 1), (1, 3), (3, 5)]
 V_COLS = [256,256,256,256,256,256,256,256,256,256]
 POOL_TILES = [(0, 1), (0, 3), (1, 1), (1, 3)]
 S_FROM = 2688
@@ -36,15 +35,13 @@ def tile_loramlp_pb_kernel(tc, h, ha, W_down, B_down, out_0, out_1):
         ha_sb = keep.tile([P, 4, R], BF16, name="ha_sb")
         nc.sync.dma_start(out=ha_sb[:], in_=ha.rearrange("(p j) r -> p j r", j=4))
         b_sb = keep.tile([P, D], BF16, name="b_sb")
-        h_of = {}
-        for n, (g0, g1) in enumerate(H_LOADS):
-            t = keep.tile([P, 4, 512 * (g1 - g0)], BF16, name="h_sb%d" % n)
-            nc.sync.dma_start(
-                out=t[:], in_=h[:, 512 * g0 : 512 * g1].rearrange("(p j) k -> p j k", j=4)
-            )
-            for g in range(g0, g1):
-                h_of[g] = (t, 512 * (g - g0))
-            if n == 0:
+        h_v = h.rearrange("(p j) k -> p j k", j=4)
+        h_sb = []
+        for j in range(4):
+            t = keep.tile([P, F], BF16, name="h_sb%d" % j)
+            nc.sync.dma_start(out=t[:], in_=h_v[:, j, :])
+            h_sb.append(t)
+            if j == 0:
                 nc.sync.dma_start(out=b_sb[:], in_=B_down)
         w_raw = []
         for g in range(PASSES):
@@ -66,11 +63,11 @@ def tile_loramlp_pb_kernel(tc, h, ha, W_down, B_down, out_0, out_1):
         lora_sb = keep.tile([P, 4, D], F32, name="lora_sb")
         out_sb = keep.tile([P, 4, D], F32, name="out_sb")
         y_sb = keep.tile([P, 4 * D], F32, name="y_sb")
-        h_codes = keep.tile([P, PASSES, 512], U32, name="h_codes", align_bytes=64)
-        h_scales = keep.tile([P, PASSES, 512], U8, name="h_scales", align_bytes=64)
+        h_codes = keep.tile([P, 4, PASSES * P], U32, name="h_codes", align_bytes=64)
+        h_scales = keep.tile([P, 4, PASSES * P], U8, name="h_scales", align_bytes=64)
         w_codes = keep.tile([P, PASSES, D], U32, name="w_codes", align_bytes=64)
         w_scales = keep.tile([P, PASSES, D], U8, name="w_scales", align_bytes=64)
-        part = keep.tile([P, 8], F32, name="part")
+        part = keep.tile([P, 4], F32, name="part")
         stat = keep.tile([P, 4], F32, name="stat")
         out0_v = out_0.rearrange("(p j) n -> p j n", j=4)
         out1_v = out_1.rearrange("(p j) n -> p j n", j=4)
@@ -89,35 +86,36 @@ def tile_loramlp_pb_kernel(tc, h, ha, W_down, B_down, out_0, out_1):
 
         hg = []
 
-        def quant_h(g):
-            nc.vector.quantize_mx(
-                out=h_codes[:, g, :].bitcast(FP8X4), scales=h_scales[:, g, :], in_=hg[g][:]
-            )
+        def quant_h(j):
+            for c0, c1 in ((0, 4 * P), (4 * P, 5 * P)):
+                nc.vector.quantize_mx(
+                    out=h_codes[:, j, c0:c1].bitcast(FP8X4),
+                    scales=h_scales[:, j, c0:c1],
+                    in_=hg[j][:, 4 * c0 : 4 * c1],
+                )
 
-        for g in range(PASSES):
-            t = keep.tile([P, 2048], BF16, name="hg%d" % g, align_bytes=64)
+        for j in range(4):
+            t = keep.tile([P, 4 * PASSES * P], BF16, name="hg%d" % j, align_bytes=64)
             hg.append(t)
-            t32 = t[:].bitcast(F32).rearrange("p (c u) -> p c u", u=2)
-            h_t, k0 = h_of[g]
-            for b in range(2):
-                xt = psum.tile([P, 2, 256], F32, tag="bank", name="xt")
-                for jj in range(2):
-                    words = h_t[:, 2 * b + jj, k0 : k0 + 512].bitcast(F32)
+            t32 = t[:].bitcast(F32).rearrange("p (g r u) -> p g r u", r=P, u=2)
+            words = h_sb[j][:].bitcast(F32)
+            for n, (g0, g1) in enumerate(((0, 2), (2, 4), (4, 5))):
+                xt = psum.tile([P, g1 - g0, 2, P], F32, tag="bank", name="xt")
+                for g in range(g0, g1):
                     for u in range(2):
                         nc.tensor.transpose(
-                            xt[:, u, P * jj : P * (jj + 1)], words[:, u:256:2], ident_f[:]
+                            xt[:, g - g0, u, :], words[:, 256 * g + u : 256 * (g + 1) : 2], ident_f[:]
                         )
-                dst = t32[:, 256 * b : 256 * (b + 1), :]
-                src = xt[:].rearrange("p u r -> p r u")
-                if b == 0:
-                    nc.vector.tensor_copy(out=dst, in_=src)
-                else:
+                dst = t32[:, g0:g1, :, :]
+                src = xt[:].rearrange("p g u r -> p g r u")
+                if n == 1:
                     nc.scalar.copy(out=dst, in_=src)
-            if g > 0:
-                quant_h(g - 1)
-            for l in (2 * g, 2 * g + 1):
-                if l < 8:
-                    lora(l)
+                else:
+                    nc.vector.tensor_copy(out=dst, in_=src)
+            if j > 0:
+                quant_h(j - 1)
+            lora(2 * j)
+            lora(2 * j + 1)
 
         chunks = [(g, half) for g in range(PASSES) for half in range(2)]
         acc = {}
@@ -143,11 +141,11 @@ def tile_loramlp_pb_kernel(tc, h, ha, W_down, B_down, out_0, out_1):
             for j in range(4):
                 if g == 0:
                     acc[(half, j)] = psum.tile([P, NH], F32, tag="bank", name="acc%d%d" % (half, j))
-                tok = slice(P * j, P * (j + 1))
+                tok = slice(P * g, P * (g + 1))
                 nc.tensor.matmul_mx(
                     out=acc[(half, j)][:],
-                    lhsT=h_codes[:, g, tok].bitcast(FP8X4),
-                    lhsT_scale=h_scales[:, g, tok],
+                    lhsT=h_codes[:, j, tok].bitcast(FP8X4),
+                    lhsT_scale=h_scales[:, j, tok],
                     rhs=w_codes[:, g, cols].bitcast(FP8X4),
                     rhs_scale=w_scales[:, g, cols],
                     start=(g == 0),
@@ -155,7 +153,7 @@ def tile_loramlp_pb_kernel(tc, h, ha, W_down, B_down, out_0, out_1):
                 )
 
         interleave(0)
-        quant_h(PASSES - 1)
+        quant_h(3)
         for i in range(1, len(chunks)):
             interleave(i)
             quant_mm(i - 1)
@@ -179,25 +177,23 @@ def tile_loramlp_pb_kernel(tc, h, ha, W_down, B_down, out_0, out_1):
             nc.vector.tensor_tensor(out=o, in0=acc[(half, j)][:], in1=lo, op=ALU.add)
             store0(half, j)
 
-        def red(half, j):
-            o, lo = tile_of(half, j)
-            l = 4 * half + j
+        def red(j):
             nc.vector.tensor_reduce(
-                out=part[:, l : l + 1], in_=o, axis=AX.X, op=ALU.max, apply_absolute_value=True
+                out=part[:, j : j + 1], in_=out_sb[:, j, :], axis=AX.X, op=ALU.max, apply_absolute_value=True
             )
 
-        tiles = [(half, j) for half in range(2) for j in range(4)]
         for t in POOL_TILES:
             pool_add(t[0], t[1])
-        mine = [t for t in tiles if t not in POOL_TILES]
-        add(mine[0][0], mine[0][1])
-        for n in range(1, len(mine)):
-            add(mine[n][0], mine[n][1])
-            red(mine[n - 1][0], mine[n - 1][1])
-        red(mine[-1][0], mine[-1][1])
+        add(0, 0)
+        add(0, 2)
+        add(1, 0)
+        add(1, 2)
+        red(0)
+        red(2)
         for t in POOL_TILES:
             store0(t[0], t[1])
-            red(t[0], t[1])
+        red(1)
+        red(3)
 
         nc.vector.tensor_reduce(out=stat[:, 0:1], in_=part[:], axis=AX.X, op=ALU.max)
         am_ps = psum.tile([P, P], F32, tag="bank", name="am_ps")

@@ -58,11 +58,12 @@ def tile_loramlp_pb_kernel(tc, h, ha, W_down, B_down, out_0, out_1):
         warm = keep.tile([P, 2], F32, name="warm")
         nc.vector.memset(warm[:, 0:1], 0.0)
         nc.scalar.activation(out=warm[:, 1:2], in_=warm[:, 0:1], func=ACT.Copy)
+        zero = keep.tile([P, 1], F32, name="zero")
+        nc.vector.memset(zero[:], 0.0)
 
         haT = keep.tile([P, 4, P], BF16, name="haT")
         lora_sb = keep.tile([P, 4, D], F32, name="lora_sb")
         out_sb = keep.tile([P, 4, D], F32, name="out_sb")
-        y_sb = keep.tile([P, 4 * D], F32, name="y_sb")
         h_codes = keep.tile([P, 4, PASSES * P], U32, name="h_codes", align_bytes=64)
         h_scales = keep.tile([P, 4, PASSES * P], U8, name="h_scales", align_bytes=64)
         w_codes = keep.tile([P, PASSES, D], U32, name="w_codes", align_bytes=64)
@@ -200,43 +201,35 @@ def tile_loramlp_pb_kernel(tc, h, ha, W_down, B_down, out_0, out_1):
         nc.tensor.transpose(am_ps[:], stat[:, 0:1].to_broadcast([P, P]), ident_f[:])
         nc.vector.tensor_reduce(out=stat[:, 1:2], in_=am_ps[:], axis=AX.X, op=ALU.max)
         nc.vector.reciprocal(out=stat[:, 2:3], in_=stat[:, 1:2])
-        rcp = stat[:, 2:3]
+        nc.vector.tensor_scalar(out=stat[:, 3:4], in0=stat[:, 2:3], scalar1=448.0, scalar2=None, op0=ALU.mult)
+        r = stat[:, 3:4]
 
         o_flat = out_sb[:].rearrange("p j n -> p (j n)")
         f8 = [keep.tile([P, D], FP8, name="f8_%d" % j) for j in range(4)]
 
-        def v_mul(a, b):
-            nc.vector.tensor_scalar(
-                out=y_sb[:, a:b], in0=o_flat[:, a:b], scalar1=rcp, scalar2=448.0, op0=ALU.mult, op1=ALU.mult
-            )
-
-        def s_mul(a, b):
-            nc.scalar.activation(out=y_sb[:, a:b], in_=o_flat[:, a:b], func=ACT.Copy, scale=rcp)
-
         def v_cast(a, b):
             j = a // D
-            nc.vector.tensor_copy(out=f8[j][:, a - D * j : b - D * j], in_=y_sb[:, a:b], saturate=False)
+            nc.vector.tensor_scalar(
+                out=f8[j][:, a - D * j : b - D * j], in0=o_flat[:, a:b], scalar1=r, scalar2=None, op0=ALU.mult,
+                saturate=False,
+            )
 
         def s_cast(a, b):
             j = a // D
             nc.scalar.activation(
-                out=f8[j][:, a - D * j : b - D * j], in_=y_sb[:, a:b], func=ACT.Copy, scale=448.0, saturate=False
+                out=f8[j][:, a - D * j : b - D * j], in_=o_flat[:, a:b], func=ACT.Identity, scale=r,
+                bias=zero[:, 0:1], saturate=False,
             )
 
         def store(j):
             nc.sync.dma_start(out=out1_v[:, j, :], in_=f8[j][:].bitcast(U8))
 
-        s_mul(3 * D, 4 * D)
-        v_mul(0, D)
-        v_mul(D, 2 * D)
+        s_cast(3 * D, 4 * D)
         v_cast(0, D)
         store(0)
-        s_mul(S_FROM, 3 * D)
-        v_mul(2 * D, S_FROM)
         v_cast(D, 2 * D)
         store(1)
-        s_cast(3 * D, 4 * D)
         store(3)
-        v_cast(2 * D, S_FROM)
         s_cast(S_FROM, 3 * D)
+        v_cast(2 * D, S_FROM)
         store(2)

@@ -22,6 +22,7 @@ NH = 512
 V_COLS = [256,256,256,256,256,256,256,256,256,256]
 POOL_TILES = [(0, 1), (0, 3), (1, 1), (1, 3)]
 S_FROM = 2688
+N_IDLE = 6
 
 
 def tile_loramlp_pb_kernel(tc, h, ha, W_down, B_down, out_0, out_1):
@@ -36,6 +37,14 @@ def tile_loramlp_pb_kernel(tc, h, ha, W_down, B_down, out_0, out_1):
         nc.sync.dma_start(out=ha_sb[:], in_=ha.rearrange("(p j) r -> p j r", j=4))
         b_sb = keep.tile([P, D], BF16, name="b_sb")
         h_v = h.rearrange("(p j) k -> p j k", j=4)
+        w_raw = [keep.tile([P, 4, D], BF16, name="w_raw%d" % g) for g in range(PASSES)]
+
+        def w_view(g):
+            return W_down[512 * g : 512 * (g + 1), :].rearrange("(p j) w -> p j w", j=4)
+
+        for half in range(2):
+            cols = slice(NH * half, NH * (half + 1))
+            nc.sync.dma_start(out=w_raw[0][:, :, cols], in_=w_view(0)[:, :, cols])
         h_sb = []
         for j in range(4):
             t = keep.tile([P, F], BF16, name="h_sb%d" % j)
@@ -43,13 +52,8 @@ def tile_loramlp_pb_kernel(tc, h, ha, W_down, B_down, out_0, out_1):
             h_sb.append(t)
             if j == 0:
                 nc.sync.dma_start(out=b_sb[:], in_=B_down)
-        w_raw = []
-        for g in range(PASSES):
-            t = keep.tile([P, 4, D], BF16, name="w_raw%d" % g)
-            nc.sync.dma_start(
-                out=t[:], in_=W_down[512 * g : 512 * (g + 1), :].rearrange("(p j) w -> p j w", j=4)
-            )
-            w_raw.append(t)
+        for g in range(1, PASSES):
+            nc.sync.dma_start(out=w_raw[g][:], in_=w_view(g))
 
         ident_b = keep.tile([P, P], BF16, name="ident_b")
         make_identity(nc, ident_b[:])
@@ -60,23 +64,70 @@ def tile_loramlp_pb_kernel(tc, h, ha, W_down, B_down, out_0, out_1):
         nc.scalar.activation(out=warm[:, 1:2], in_=warm[:, 0:1], func=ACT.Copy)
         zero = keep.tile([P, 1], F32, name="zero")
         nc.vector.memset(zero[:], 0.0)
+        idle_rhs = keep.tile([P, NH], BF16, name="idle_rhs")
+        nc.vector.memset(idle_rhs[:], 0.0)
 
         haT = keep.tile([P, 4, P], BF16, name="haT")
         lora_sb = keep.tile([P, 4, D], F32, name="lora_sb")
-        out_sb = keep.tile([P, 4, D], F32, name="out_sb")
+        out_sb = keep.tile([P, 4 * D + 4], F32, name="out_sb")
         h_codes = keep.tile([P, 4, PASSES * P], U32, name="h_codes", align_bytes=64)
         h_scales = keep.tile([P, 4, PASSES * P], U8, name="h_scales", align_bytes=64)
         w_codes = keep.tile([P, PASSES, D], U32, name="w_codes", align_bytes=64)
         w_scales = keep.tile([P, PASSES, D], U8, name="w_scales", align_bytes=64)
-        part = keep.tile([P, 4], F32, name="part")
         stat = keep.tile([P, 4], F32, name="stat")
         out0_v = out_0.rearrange("(p j) n -> p j n", j=4)
         out1_v = out_1.rearrange("(p j) n -> p j n", j=4)
+
+        chunks = [(g, half) for g in range(PASSES) for half in range(2)]
+        acc = {}
+        wgs = {}
+
+        def interleave(i):
+            g, half = chunks[i]
+            a = V_COLS[i]
+            wg = grp.tile([P, NH, 4], BF16, tag="wg", name="wg", align_bytes=64)
+            wgs[i] = wg
+            src = w_raw[g][:, :, NH * half : NH * (half + 1)].rearrange("p t w -> p w t")
+            nc.vector.tensor_copy(out=wg[:, 0:a, :], in_=src[:, 0:a, :])
+            nc.scalar.copy(out=wg[:, a:NH, :], in_=src[:, a:NH, :])
+
+        def quant(i):
+            g, half = chunks[i]
+            cols = slice(NH * half, NH * (half + 1))
+            nc.vector.quantize_mx(
+                out=w_codes[:, g, cols].bitcast(FP8X4),
+                scales=w_scales[:, g, cols],
+                in_=wgs[i][:].rearrange("p w j -> p (w j)"),
+            )
+
+        def mm(i):
+            g, half = chunks[i]
+            cols = slice(NH * half, NH * (half + 1))
+            for j in range(4):
+                if g == 0:
+                    acc[(half, j)] = psum.tile([P, NH], F32, tag="bank", name="acc%d%d" % (half, j))
+                tok = slice(P * g, P * (g + 1))
+                nc.tensor.matmul_mx(
+                    out=acc[(half, j)][:],
+                    lhsT=h_codes[:, j, tok].bitcast(FP8X4),
+                    lhsT_scale=h_scales[:, j, tok],
+                    rhs=w_codes[:, g, cols].bitcast(FP8X4),
+                    rhs_scale=w_scales[:, g, cols],
+                    start=(g == 0),
+                    stop=(g == PASSES - 1),
+                )
 
         haT_ps = psum.tile([P, 4, P], BF16, tag="bank", name="haT_ps")
         for j in range(4):
             nc.tensor.transpose(haT_ps[:, j, :], ha_sb[:, j, :], ident_b[:])
         nc.scalar.copy(out=haT[:], in_=haT_ps[:])
+        idle_ps = psum.tile([P, NH], F32, tag="bank", name="idle_ps")
+        for n in range(N_IDLE):
+            nc.tensor.matmul(idle_ps[:], lhsT=ident_b[:], rhs=idle_rhs[:], start=True, stop=True)
+
+        interleave(0)
+        interleave(1)
+        quant(0)
 
         def lora(l):
             half, j = l // 4, l % 4
@@ -115,53 +166,25 @@ def tile_loramlp_pb_kernel(tc, h, ha, W_down, B_down, out_0, out_1):
                     nc.vector.tensor_copy(out=dst, in_=src)
             if j > 0:
                 quant_h(j - 1)
+            else:
+                quant(1)
             lora(2 * j)
             lora(2 * j + 1)
 
-        chunks = [(g, half) for g in range(PASSES) for half in range(2)]
-        acc = {}
-        wgs = {}
-
-        def interleave(i):
-            g, half = chunks[i]
-            a = V_COLS[i]
-            wg = grp.tile([P, NH, 4], BF16, tag="wg", name="wg", align_bytes=64)
-            wgs[i] = wg
-            src = w_raw[g][:, :, NH * half : NH * (half + 1)].rearrange("p t w -> p w t")
-            nc.vector.tensor_copy(out=wg[:, 0:a, :], in_=src[:, 0:a, :])
-            nc.scalar.copy(out=wg[:, a:NH, :], in_=src[:, a:NH, :])
-
-        def quant_mm(i):
-            g, half = chunks[i]
-            cols = slice(NH * half, NH * (half + 1))
-            nc.vector.quantize_mx(
-                out=w_codes[:, g, cols].bitcast(FP8X4),
-                scales=w_scales[:, g, cols],
-                in_=wgs[i][:].rearrange("p w j -> p (w j)"),
-            )
-            for j in range(4):
-                if g == 0:
-                    acc[(half, j)] = psum.tile([P, NH], F32, tag="bank", name="acc%d%d" % (half, j))
-                tok = slice(P * g, P * (g + 1))
-                nc.tensor.matmul_mx(
-                    out=acc[(half, j)][:],
-                    lhsT=h_codes[:, j, tok].bitcast(FP8X4),
-                    lhsT_scale=h_scales[:, j, tok],
-                    rhs=w_codes[:, g, cols].bitcast(FP8X4),
-                    rhs_scale=w_scales[:, g, cols],
-                    start=(g == 0),
-                    stop=(g == PASSES - 1),
-                )
-
-        interleave(0)
+        interleave(2)
         quant_h(3)
-        for i in range(1, len(chunks)):
+        mm(0)
+        mm(1)
+        for i in range(3, len(chunks)):
             interleave(i)
-            quant_mm(i - 1)
-        quant_mm(len(chunks) - 1)
+            quant(i - 1)
+            mm(i - 1)
+        quant(len(chunks) - 1)
+        mm(len(chunks) - 1)
 
         def tile_of(half, j):
-            return out_sb[:, j, NH * half : NH * (half + 1)], lora_sb[:, j, NH * half : NH * (half + 1)]
+            c0 = D * j + NH * half
+            return out_sb[:, c0 : c0 + NH], lora_sb[:, j, NH * half : NH * (half + 1)]
 
         def store0(half, j):
             o, lo = tile_of(half, j)
@@ -178,9 +201,10 @@ def tile_loramlp_pb_kernel(tc, h, ha, W_down, B_down, out_0, out_1):
             nc.vector.tensor_tensor(out=o, in0=acc[(half, j)][:], in1=lo, op=ALU.add)
             store0(half, j)
 
-        def red(j):
+        def red(j, n):
             nc.vector.tensor_reduce(
-                out=part[:, j : j + 1], in_=out_sb[:, j, :], axis=AX.X, op=ALU.max, apply_absolute_value=True
+                out=out_sb[:, 4 * D + n : 4 * D + n + 1], in_=out_sb[:, D * j : D * (j + 1)], axis=AX.X, op=ALU.max,
+                apply_absolute_value=True,
             )
 
         for t in POOL_TILES:
@@ -189,14 +213,15 @@ def tile_loramlp_pb_kernel(tc, h, ha, W_down, B_down, out_0, out_1):
         add(0, 2)
         add(1, 0)
         add(1, 2)
-        red(0)
-        red(2)
+        red(0, 0)
+        red(2, 1)
         for t in POOL_TILES:
             store0(t[0], t[1])
-        red(1)
-        red(3)
+        red(1, 2)
+        nc.vector.tensor_reduce(
+            out=stat[:, 0:1], in_=out_sb[:, 3 * D : 4 * D + 3], axis=AX.X, op=ALU.max, apply_absolute_value=True
+        )
 
-        nc.vector.tensor_reduce(out=stat[:, 0:1], in_=part[:], axis=AX.X, op=ALU.max)
         am_ps = psum.tile([P, P], F32, tag="bank", name="am_ps")
         nc.tensor.transpose(am_ps[:], stat[:, 0:1].to_broadcast([P, P]), ident_f[:])
         nc.vector.tensor_reduce(out=stat[:, 1:2], in_=am_ps[:], axis=AX.X, op=ALU.max)
@@ -204,7 +229,7 @@ def tile_loramlp_pb_kernel(tc, h, ha, W_down, B_down, out_0, out_1):
         nc.vector.tensor_scalar(out=stat[:, 3:4], in0=stat[:, 2:3], scalar1=448.0, scalar2=None, op0=ALU.mult)
         r = stat[:, 3:4]
 
-        o_flat = out_sb[:].rearrange("p j n -> p (j n)")
+        o_flat = out_sb
         f8 = [keep.tile([P, D], FP8, name="f8_%d" % j) for j in range(4)]
 
         def v_cast(a, b):

@@ -21,6 +21,7 @@ PASSES = F // 512
 NH = 512
 V_COLS = [256,256,256,256,256,256,256,256,256,256]
 POOL_TILES = [(0, 1), (0, 3), (1, 1), (1, 3)]
+PE_TILES = [(1, 0), (1, 2)]
 S_FROM = 2688
 N_IDLE = 6
 
@@ -69,7 +70,7 @@ def tile_loramlp_pb_kernel(tc, h, ha, W_down, B_down, out_0, out_1):
 
         haT = keep.tile([P, 4, P], BF16, name="haT")
         lora_sb = keep.tile([P, 4, D], F32, name="lora_sb")
-        out_sb = keep.tile([P, 4 * D + 4], F32, name="out_sb")
+        out_sb = keep.tile([P, 4 * D + 8], F32, name="out_sb")
         h_codes = keep.tile([P, 4, PASSES * P], U32, name="h_codes", align_bytes=64)
         h_scales = keep.tile([P, 4, PASSES * P], U8, name="h_scales", align_bytes=64)
         w_codes = keep.tile([P, PASSES, D], U32, name="w_codes", align_bytes=64)
@@ -131,6 +132,8 @@ def tile_loramlp_pb_kernel(tc, h, ha, W_down, B_down, out_0, out_1):
 
         def lora(l):
             half, j = l // 4, l % 4
+            if (half, j) in PE_TILES:
+                return
             cols = slice(NH * half, NH * (half + 1))
             lp = psum.tile([P, NH], F32, tag="bank", name="lora_ps")
             nc.tensor.matmul(lp[:], lhsT=haT[:, j, :], rhs=b_sb[:, cols], start=True, stop=True)
@@ -201,25 +204,58 @@ def tile_loramlp_pb_kernel(tc, h, ha, W_down, B_down, out_0, out_1):
             nc.vector.tensor_tensor(out=o, in0=acc[(half, j)][:], in1=lo, op=ALU.add)
             store0(half, j)
 
-        def red(j, n):
+        def red(half, j, n):
+            c0 = D * j + NH * half
             nc.vector.tensor_reduce(
-                out=out_sb[:, 4 * D + n : 4 * D + n + 1], in_=out_sb[:, D * j : D * (j + 1)], axis=AX.X, op=ALU.max,
+                out=out_sb[:, 4 * D + n : 4 * D + n + 1], in_=out_sb[:, c0 : c0 + NH], axis=AX.X, op=ALU.max,
                 apply_absolute_value=True,
             )
 
-        for t in POOL_TILES:
-            pool_add(t[0], t[1])
+        both = {}
+        mxs = {}
+
+        def pe_open(half, j):
+            both[(half, j)] = psum.tile([P, NH], F32, tag="bank", name="both%d%d" % (half, j))
+            nc.tensor.matmul(
+                both[(half, j)][:], lhsT=haT[:, j, :], rhs=b_sb[:, NH * half : NH * (half + 1)], start=True, stop=False
+            )
+
+        def pe_in(half, j):
+            mxs[(half, j)] = keep.tile([P, NH], F32, name="mx%d%d" % (half, j))
+            nc.scalar.copy(out=mxs[(half, j)][:], in_=acc[(half, j)][:])
+            nc.tensor.matmul(both[(half, j)][:], lhsT=ident_f[:], rhs=mxs[(half, j)][:], start=False, stop=True)
+
+        def pe_out(half, j):
+            o, lo = tile_of(half, j)
+            nc.scalar.copy(out=o, in_=both[(half, j)][:])
+
+        pool_add(0, 1)
+        pool_add(0, 3)
         add(0, 0)
         add(0, 2)
-        add(1, 0)
-        add(1, 2)
-        red(0, 0)
-        red(2, 1)
-        for t in POOL_TILES:
-            store0(t[0], t[1])
-        red(1, 2)
+        pe_open(1, 0)
+        pe_open(1, 2)
+        pe_in(1, 0)
+        pool_add(1, 1)
+        pe_in(1, 2)
+        pe_out(1, 0)
+        pool_add(1, 3)
+        pe_out(1, 2)
+        red(0, 0, 0)
+        red(0, 2, 1)
+        store0(0, 1)
+        red(0, 1, 2)
+        store0(0, 3)
+        red(0, 3, 3)
+        store0(1, 0)
+        red(1, 0, 4)
+        store0(1, 1)
+        red(1, 1, 5)
+        store0(1, 2)
+        red(1, 2, 6)
+        store0(1, 3)
         nc.vector.tensor_reduce(
-            out=stat[:, 0:1], in_=out_sb[:, 3 * D : 4 * D + 3], axis=AX.X, op=ALU.max, apply_absolute_value=True
+            out=stat[:, 0:1], in_=out_sb[:, 3 * D + NH : 4 * D + 7], axis=AX.X, op=ALU.max, apply_absolute_value=True
         )
 
         am_ps = psum.tile([P, P], F32, tag="bank", name="am_ps")

@@ -19,7 +19,7 @@ AX = mybir.AxisListType
 P = 128
 PASSES = F // 512
 NH = 512
-V_COLS = [256,256,256,256,256,256,256,256,256,256]
+V_COLS = [256, 256, 264, 264, 264, 264, 264, 264, 264, 264]
 POOL_TILES = [(0, 1), (0, 3), (1, 1), (1, 3)]
 PE_TILES = [(1, 0), (1, 2)]
 S_FROM = 2688
@@ -163,7 +163,7 @@ def tile_loramlp_pb_kernel(tc, h, ha, W_down, B_down, out_0, out_1):
                         )
                 dst = t32[:, g0:g1, :, :]
                 src = xt[:].rearrange("p g u r -> p g r u")
-                if n == 1:
+                if n > 0:
                     nc.scalar.copy(out=dst, in_=src)
                 else:
                     nc.vector.tensor_copy(out=dst, in_=src)

@@ -19,11 +19,10 @@ AX = mybir.AxisListType
 P = 128
 PASSES = F // 512
 NH = 512
-V_COLS = [256, 256, 264, 264, 264, 264, 264, 264, 264, 264]
+V_COLS = [264, 264, 264, 264, 264, 264, 264, 264, 264, 264]
 POOL_TILES = [(0, 1), (0, 3), (1, 1), (1, 3)]
 PE_TILES = [(1, 0), (1, 2)]
 S_FROM = 2688
-N_IDLE = 6
 
 
 def tile_loramlp_pb_kernel(tc, h, ha, W_down, B_down, out_0, out_1):
@@ -43,9 +42,6 @@ def tile_loramlp_pb_kernel(tc, h, ha, W_down, B_down, out_0, out_1):
         def w_view(g):
             return W_down[512 * g : 512 * (g + 1), :].rearrange("(p j) w -> p j w", j=4)
 
-        for half in range(2):
-            cols = slice(NH * half, NH * (half + 1))
-            nc.sync.dma_start(out=w_raw[0][:, :, cols], in_=w_view(0)[:, :, cols])
         h_sb = []
         for j in range(4):
             t = keep.tile([P, F], BF16, name="h_sb%d" % j)
@@ -53,7 +49,7 @@ def tile_loramlp_pb_kernel(tc, h, ha, W_down, B_down, out_0, out_1):
             h_sb.append(t)
             if j == 0:
                 nc.sync.dma_start(out=b_sb[:], in_=B_down)
-        for g in range(1, PASSES):
+        for g in range(PASSES):
             nc.sync.dma_start(out=w_raw[g][:], in_=w_view(g))
 
         ident_b = keep.tile([P, P], BF16, name="ident_b")
@@ -65,8 +61,6 @@ def tile_loramlp_pb_kernel(tc, h, ha, W_down, B_down, out_0, out_1):
         nc.scalar.activation(out=warm[:, 1:2], in_=warm[:, 0:1], func=ACT.Copy)
         zero = keep.tile([P, 1], F32, name="zero")
         nc.vector.memset(zero[:], 0.0)
-        idle_rhs = keep.tile([P, NH], BF16, name="idle_rhs")
-        nc.vector.memset(idle_rhs[:], 0.0)
 
         haT = keep.tile([P, 4, P], BF16, name="haT")
         lora_sb = keep.tile([P, 4, D], F32, name="lora_sb")
@@ -122,13 +116,6 @@ def tile_loramlp_pb_kernel(tc, h, ha, W_down, B_down, out_0, out_1):
         for j in range(4):
             nc.tensor.transpose(haT_ps[:, j, :], ha_sb[:, j, :], ident_b[:])
         nc.scalar.copy(out=haT[:], in_=haT_ps[:])
-        idle_ps = psum.tile([P, NH], F32, tag="bank", name="idle_ps")
-        for n in range(N_IDLE):
-            nc.tensor.matmul(idle_ps[:], lhsT=ident_b[:], rhs=idle_rhs[:], start=True, stop=True)
-
-        interleave(0)
-        interleave(1)
-        quant(0)
 
         def lora(l):
             half, j = l // 4, l % 4
@@ -169,16 +156,12 @@ def tile_loramlp_pb_kernel(tc, h, ha, W_down, B_down, out_0, out_1):
                     nc.vector.tensor_copy(out=dst, in_=src)
             if j > 0:
                 quant_h(j - 1)
-            else:
-                quant(1)
             lora(2 * j)
             lora(2 * j + 1)
 
-        interleave(2)
+        interleave(0)
         quant_h(3)
-        mm(0)
-        mm(1)
-        for i in range(3, len(chunks)):
+        for i in range(1, len(chunks)):
             interleave(i)
             quant(i - 1)
             mm(i - 1)

@@ -23,6 +23,7 @@ V_COLS = [264, 264, 264, 264, 264, 264, 264, 264, 264, 264]
 POOL_TILES = [(0, 1), (0, 3), (1, 1), (1, 3)]
 PE_TILES = [(1, 0), (1, 2)]
 S_FROM = 2688
+N_IDLE = 6
 
 
 def tile_loramlp_pb_kernel(tc, h, ha, W_down, B_down, out_0, out_1):
@@ -61,6 +62,8 @@ def tile_loramlp_pb_kernel(tc, h, ha, W_down, B_down, out_0, out_1):
         nc.scalar.activation(out=warm[:, 1:2], in_=warm[:, 0:1], func=ACT.Copy)
         zero = keep.tile([P, 1], F32, name="zero")
         nc.vector.memset(zero[:], 0.0)
+        idle_rhs = keep.tile([P, NH], BF16, name="idle_rhs")
+        nc.vector.memset(idle_rhs[:], 0.0)
 
         haT = keep.tile([P, 4, P], BF16, name="haT")
         lora_sb = keep.tile([P, 4, D], F32, name="lora_sb")
@@ -224,6 +227,9 @@ def tile_loramlp_pb_kernel(tc, h, ha, W_down, B_down, out_0, out_1):
         pe_out(1, 0)
         pool_add(1, 3)
         pe_out(1, 2)
+        idle_ps = psum.tile([P, NH], F32, tag="bank", name="idle_ps")
+        for n in range(N_IDLE):
+            nc.tensor.matmul(idle_ps[:], lhsT=ident_b[:], rhs=idle_rhs[:], start=True, stop=True)
         red(0, 0, 0)
         red(0, 2, 1)
         store0(0, 1)

@@ -20,8 +20,8 @@ P = 128
 PASSES = F // 512
 NH = 512
 V_COLS = [264, 264, 264, 264, 264, 264, 264, 264, 264, 264]
-POOL_TILES = [(0, 1), (0, 3), (1, 1), (1, 3)]
-PE_TILES = [(1, 0), (1, 2)]
+POOL_TILES = [(0, 1), (0, 3), (1, 1)]
+PE_TILES = [(1, 2), (1, 3)]
 S_FROM = 2688
 N_IDLE = 6
 
@@ -219,29 +219,28 @@ def tile_loramlp_pb_kernel(tc, h, ha, W_down, B_down, out_0, out_1):
         pool_add(0, 3)
         add(0, 0)
         add(0, 2)
-        pe_open(1, 0)
+        add(1, 0)
         pe_open(1, 2)
-        pe_in(1, 0)
+        pe_open(1, 3)
         pool_add(1, 1)
         pe_in(1, 2)
-        pe_out(1, 0)
-        pool_add(1, 3)
+        pe_in(1, 3)
         pe_out(1, 2)
+        pe_out(1, 3)
         idle_ps = psum.tile([P, NH], F32, tag="bank", name="idle_ps")
         for n in range(N_IDLE):
             nc.tensor.matmul(idle_ps[:], lhsT=ident_b[:], rhs=idle_rhs[:], start=True, stop=True)
         red(0, 0, 0)
         red(0, 2, 1)
+        red(1, 0, 2)
         store0(0, 1)
-        red(0, 1, 2)
+        red(0, 1, 3)
         store0(0, 3)
-        red(0, 3, 3)
-        store0(1, 0)
-        red(1, 0, 4)
-        store0(1, 1)
-        red(1, 1, 5)
+        red(0, 3, 4)
         store0(1, 2)
-        red(1, 2, 6)
+        red(1, 2, 5)
+        store0(1, 1)
+        red(1, 1, 6)
         store0(1, 3)
         nc.vector.tensor_reduce(
             out=stat[:, 0:1], in_=out_sb[:, 3 * D + NH : 4 * D + 7], axis=AX.X, op=ALU.max, apply_absolute_value=True

@@ -130,9 +130,10 @@ def tile_loramlp_pb_kernel(tc, h, ha, W_down, B_down, out_0, out_1):
             nc.scalar.copy(out=lora_sb[:, j, cols], in_=lp[:])
 
         hg = []
+        late = []
 
-        def quant_h(j):
-            for c0, c1 in ((0, 4 * P), (4 * P, 5 * P)):
+        def quant_h(j, parts=((0, 4 * P), (4 * P, 5 * P))):
+            for c0, c1 in parts:
                 nc.vector.quantize_mx(
                     out=h_codes[:, j, c0:c1].bitcast(FP8X4),
                     scales=h_scales[:, j, c0:c1],
@@ -153,7 +154,9 @@ def tile_loramlp_pb_kernel(tc, h, ha, W_down, B_down, out_0, out_1):
                         )
                 dst = t32[:, g0:g1, :, :]
                 src = xt[:].rearrange("p g u r -> p g r u")
-                if n > 0:
+                if n == 2 and j == 3:
+                    late.append((dst, src))
+                elif n > 0:
                     nc.scalar.copy(out=dst, in_=src)
                 else:
                     nc.vector.tensor_copy(out=dst, in_=src)
@@ -163,11 +166,17 @@ def tile_loramlp_pb_kernel(tc, h, ha, W_down, B_down, out_0, out_1):
             lora(2 * j + 1)
 
         interleave(0)
-        quant_h(3)
-        for i in range(1, len(chunks)):
+        nc.scalar.copy(out=late[0][0], in_=late[0][1])
+        interleave(1)
+        quant_h(3, ((0, 4 * P),))
+        quant(0)
+        mm(0)
+        for i in range(2, len(chunks)):
             interleave(i)
             quant(i - 1)
             mm(i - 1)
+            if i == 4:
+                quant_h(3, ((4 * P, 5 * P),))
         quant(len(chunks) - 1)
         mm(len(chunks) - 1)
 
@@ -248,9 +257,12 @@ def tile_loramlp_pb_kernel(tc, h, ha, W_down, B_down, out_0, out_1):
 
         am_ps = psum.tile([P, P], F32, tag="bank", name="am_ps")
         nc.tensor.transpose(am_ps[:], stat[:, 0:1].to_broadcast([P, P]), ident_f[:])
-        nc.vector.tensor_reduce(out=stat[:, 1:2], in_=am_ps[:], axis=AX.X, op=ALU.max)
-        nc.vector.reciprocal(out=stat[:, 2:3], in_=stat[:, 1:2])
-        nc.vector.tensor_scalar(out=stat[:, 3:4], in0=stat[:, 2:3], scalar1=448.0, scalar2=None, op0=ALU.mult)
+        am_sb = keep.tile([P, P], F32, name="am_sb")
+        nc.vector.tensor_scalar(
+            out=am_sb[:], in0=am_ps[:], scalar1=1.0 / 448.0, scalar2=None, op0=ALU.mult, op1=ALU.max,
+            accum_out=stat[:, 1:2],
+        )
+        nc.vector.reciprocal(out=stat[:, 3:4], in_=stat[:, 1:2])
         r = stat[:, 3:4]
 
         o_flat = out_sb

@@ -85,9 +85,15 @@ def tile_loramlp_pb_kernel(tc, h, ha, W_down, B_down, out_0, out_1):
             a = V_COLS[i]
             wg = grp.tile([P, NH, 4], BF16, tag="wg", name="wg", align_bytes=64)
             wgs[i] = wg
-            src = w_raw[g][:, :, NH * half : NH * (half + 1)].rearrange("p t w -> p w t")
-            nc.vector.tensor_copy(out=wg[:, 0:a, :], in_=src[:, 0:a, :])
-            nc.scalar.copy(out=wg[:, a:NH, :], in_=src[:, a:NH, :])
+            c0 = NH * half
+            nc.vector.tensor_copy(
+                out=wg[:, 0:a, :].rearrange("p (c i) t -> p c t i", i=4),
+                in_=w_raw[g][:, :, c0 : c0 + a].rearrange("p t (c i) -> p c t i", i=4),
+            )
+            nc.scalar.copy(
+                out=wg[:, a:NH, :].rearrange("p (c i) t -> p c t i", i=4),
+                in_=w_raw[g][:, :, c0 + a : c0 + NH].rearrange("p t (c i) -> p c t i", i=4),
+            )
 
         def quant(i):
             g, half = chunks[i]

@@ -19,7 +19,7 @@ AX = mybir.AxisListType
 P = 128
 PASSES = F // 512
 NH = 512
-V_COLS = [264, 264, 264, 264, 264, 264, 264, 264, 264, 264]
+V_COLS = [264, 264, 240, 240, 240, 240, 240, 240, 240, 240]
 POOL_TILES = [(0, 1), (0, 3), (1, 1)]
 PE_TILES = [(1, 2), (1, 3)]
 S_FROM = 2688
@@ -104,10 +104,10 @@ def tile_loramlp_pb_kernel(tc, h, ha, W_down, B_down, out_0, out_1):
                 in_=wgs[i][:].rearrange("p w j -> p (w j)"),
             )
 
-        def mm(i):
+        def mm(i, order=(0, 1, 2, 3)):
             g, half = chunks[i]
             cols = slice(NH * half, NH * (half + 1))
-            for j in range(4):
+            for j in order:
                 if g == 0:
                     acc[(half, j)] = psum.tile([P, NH], F32, tag="bank", name="acc%d%d" % (half, j))
                 tok = slice(P * g, P * (g + 1))
@@ -180,11 +180,11 @@ def tile_loramlp_pb_kernel(tc, h, ha, W_down, B_down, out_0, out_1):
         for i in range(2, len(chunks)):
             interleave(i)
             quant(i - 1)
-            mm(i - 1)
+            mm(i - 1, (1, 0, 3, 2) if i == 9 else (0, 1, 2, 3))
             if i == 4:
                 quant_h(3, ((4 * P, 5 * P),))
         quant(len(chunks) - 1)
-        mm(len(chunks) - 1)
+        mm(len(chunks) - 1, (2, 3, 0, 1))
 
         def tile_of(half, j):
             c0 = D * j + NH * half
@@ -234,12 +234,12 @@ def tile_loramlp_pb_kernel(tc, h, ha, W_down, B_down, out_0, out_1):
         pool_add(0, 3)
         add(0, 0)
         add(0, 2)
-        add(1, 0)
         pe_open(1, 2)
         pe_open(1, 3)
-        pool_add(1, 1)
         pe_in(1, 2)
         pe_in(1, 3)
+        add(1, 0)
+        pool_add(1, 1)
         pe_out(1, 2)
         pe_out(1, 3)
         idle_ps = psum.tile([P, NH], F32, tag="bank", name="idle_ps")

@@ -19,7 +19,7 @@ AX = mybir.AxisListType
 P = 128
 PASSES = F // 512
 NH = 512
-V_COLS = [264, 264, 240, 240, 240, 240, 240, 240, 240, 240]
+V_COLS = [256, 256, 240, 240, 240, 240, 240, 240, 240, 240]
 POOL_TILES = [(0, 1), (0, 3), (1, 1)]
 PE_TILES = [(1, 2), (1, 3)]
 S_FROM = 2688
@@ -87,12 +87,12 @@ def tile_loramlp_pb_kernel(tc, h, ha, W_down, B_down, out_0, out_1):
             wgs[i] = wg
             c0 = NH * half
             nc.vector.tensor_copy(
-                out=wg[:, 0:a, :].rearrange("p (c i) t -> p c t i", i=4),
-                in_=w_raw[g][:, :, c0 : c0 + a].rearrange("p t (c i) -> p c t i", i=4),
+                out=wg[:, 0:a, :].rearrange("p (c i) t -> p c t i", i=8),
+                in_=w_raw[g][:, :, c0 : c0 + a].rearrange("p t (c i) -> p c t i", i=8),
             )
             nc.scalar.copy(
-                out=wg[:, a:NH, :].rearrange("p (c i) t -> p c t i", i=4),
-                in_=w_raw[g][:, :, c0 + a : c0 + NH].rearrange("p t (c i) -> p c t i", i=4),
+                out=wg[:, a:NH, :].rearrange("p (c i) t -> p c t i", i=8),
+                in_=w_raw[g][:, :, c0 + a : c0 + NH].rearrange("p t (c i) -> p c t i", i=8),
             )
 
         def quant(i):

@@ -180,7 +180,7 @@ def tile_loramlp_pb_kernel(tc, h, ha, W_down, B_down, out_0, out_1):
         for i in range(2, len(chunks)):
             interleave(i)
             quant(i - 1)
-            mm(i - 1, (1, 0, 3, 2) if i == 9 else (0, 1, 2, 3))
+            mm(i - 1)
             if i == 4:
                 quant_h(3, ((4 * P, 5 * P),))
         quant(len(chunks) - 1)
@@ -234,6 +234,8 @@ def tile_loramlp_pb_kernel(tc, h, ha, W_down, B_down, out_0, out_1):
         pool_add(0, 3)
         add(0, 0)
         add(0, 2)
+        red(0, 0, 0)
+        red(0, 2, 1)
         pe_open(1, 2)
         pe_open(1, 3)
         pe_in(1, 2)
@@ -245,11 +247,9 @@ def tile_loramlp_pb_kernel(tc, h, ha, W_down, B_down, out_0, out_1):
         idle_ps = psum.tile([P, NH], F32, tag="bank", name="idle_ps")
         for n in range(N_IDLE):
             nc.tensor.matmul(idle_ps[:], lhsT=ident_b[:], rhs=idle_rhs[:], start=True, stop=True)
-        red(0, 0, 0)
-        red(0, 2, 1)
-        red(1, 0, 2)
         store0(0, 1)
-        red(0, 1, 3)
+        red(0, 1, 2)
+        red(1, 0, 3)
         store0(0, 3)
         red(0, 3, 4)
         store0(1, 2)

@@ -177,14 +177,20 @@ def tile_loramlp_pb_kernel(tc, h, ha, W_down, B_down, out_0, out_1):
         quant_h(3, ((0, 4 * P),))
         quant(0)
         mm(0)
-        for i in range(2, len(chunks)):
+        for i in range(2, 8):
             interleave(i)
             quant(i - 1)
             mm(i - 1)
             if i == 4:
                 quant_h(3, ((4 * P, 5 * P),))
-        quant(len(chunks) - 1)
-        mm(len(chunks) - 1, (2, 3, 0, 1))
+        quant(7)
+        mm(7)
+        interleave(8)
+        interleave(9)
+        quant(8)
+        mm(8)
+        quant(9)
+        mm(9, (2, 3, 0, 1))
 
         def tile_of(half, j):
             c0 = D * j + NH * half

from contextlib import ExitStack

import concourse.mybir as mybir
from concourse.masks import make_identity

T, D, F, R = 512, 1024, 2560, 128
FLOPS = 2 * T * F * D + 2 * T * R * D

F32 = mybir.dt.float32
BF16 = mybir.dt.bfloat16
U32 = mybir.dt.uint32
U8 = mybir.dt.uint8
FP8X4 = mybir.dt.float8_e4m3fn_x4
FP8 = mybir.dt.float8_e4m3fn
ALU = mybir.AluOpType
ACT = mybir.ActivationFunctionType
AX = mybir.AxisListType

P = 128
PASSES = F // 512
NH = 512
V_COLS = [256, 256, 240, 240, 240, 240, 240, 240, 240, 240]
POOL_TILES = [(0, 1), (0, 3), (1, 1)]
PE_TILES = [(1, 2), (1, 3)]
S_FROM = 2688
N_IDLE = 6


def tile_loramlp_pb_kernel(tc, h, ha, W_down, B_down, out_0, out_1):
    nc = tc.nc
    with ExitStack() as ctx:
        keep = ctx.enter_context(tc.tile_pool(name="keep", bufs=1))
        grp = ctx.enter_context(tc.tile_pool(name="grp", bufs=4))
        psum = ctx.enter_context(tc.psum_pool(name="psum", bufs=8))
        ctx.enter_context(tc.manual_schedule())

        ha_sb = keep.tile([P, 4, R], BF16, name="ha_sb")
        nc.sync.dma_start(out=ha_sb[:], in_=ha.rearrange("(p j) r -> p j r", j=4))
        b_sb = keep.tile([P, D], BF16, name="b_sb")
        h_v = h.rearrange("(p j) k -> p j k", j=4)
        w_raw = [keep.tile([P, 4, D], BF16, name="w_raw%d" % g) for g in range(PASSES)]

        def w_view(g):
            return W_down[512 * g : 512 * (g + 1), :].rearrange("(p j) w -> p j w", j=4)

        h_sb = []
        for j in range(4):
            t = keep.tile([P, F], BF16, name="h_sb%d" % j)
            nc.sync.dma_start(out=t[:], in_=h_v[:, j, :])
            h_sb.append(t)
            if j == 0:
                nc.sync.dma_start(out=b_sb[:], in_=B_down)
        for g in range(PASSES):
            nc.sync.dma_start(out=w_raw[g][:], in_=w_view(g))

        ident_b = keep.tile([P, P], BF16, name="ident_b")
        make_identity(nc, ident_b[:])
        ident_f = keep.tile([P, P], F32, name="ident_f")
        make_identity(nc, ident_f[:])
        warm = keep.tile([P, 2], F32, name="warm")
        nc.vector.memset(warm[:, 0:1], 0.0)
        nc.scalar.activation(out=warm[:, 1:2], in_=warm[:, 0:1], func=ACT.Copy)
        zero = keep.tile([P, 1], F32, name="zero")
        nc.vector.memset(zero[:], 0.0)
        idle_rhs = keep.tile([P, NH], BF16, name="idle_rhs")
        nc.vector.memset(idle_rhs[:], 0.0)

        haT = keep.tile([P, 4, P], BF16, name="haT")
        lora_sb = keep.tile([P, 4, D], F32, name="lora_sb")
        out_sb = keep.tile([P, 4 * D + 8], F32, name="out_sb")
        h_codes = keep.tile([P, 4, PASSES * P], U32, name="h_codes", align_bytes=64)
        h_scales = keep.tile([P, 4, PASSES * P], U8, name="h_scales", align_bytes=64)
        w_codes = keep.tile([P, PASSES, D], U32, name="w_codes", align_bytes=64)
        w_scales = keep.tile([P, PASSES, D], U8, name="w_scales", align_bytes=64)
        stat = keep.tile([P, 4], F32, name="stat")
        out0_v = out_0.rearrange("(p j) n -> p j n", j=4)
        out1_v = out_1.rearrange("(p j) n -> p j n", j=4)

        chunks = [(g, half) for g in range(PASSES) for half in range(2)]
        acc = {}
        wgs = {}

        def interleave(i):
            g, half = chunks[i]
            a = V_COLS[i]
            wg = grp.tile([P, NH, 4], BF16, tag="wg", name="wg", align_bytes=64)
            wgs[i] = wg
            c0 = NH * half
            nc.vector.tensor_copy(
                out=wg[:, 0:a, :].rearrange("p (c i) t -> p c t i", i=8),
                in_=w_raw[g][:, :, c0 : c0 + a].rearrange("p t (c i) -> p c t i", i=8),
            )
            nc.scalar.copy(
                out=wg[:, a:NH, :].rearrange("p (c i) t -> p c t i", i=8),
                in_=w_raw[g][:, :, c0 + a : c0 + NH].rearrange("p t (c i) -> p c t i", i=8),
            )

        def quant(i):
            g, half = chunks[i]
            cols = slice(NH * half, NH * (half + 1))
            nc.vector.quantize_mx(
                out=w_codes[:, g, cols].bitcast(FP8X4),
                scales=w_scales[:, g, cols],
                in_=wgs[i][:].rearrange("p w j -> p (w j)"),
            )

        def mm(i, order=(0, 1, 2, 3)):
            g, half = chunks[i]
            cols = slice(NH * half, NH * (half + 1))
            for j in order:
                if g == 0:
                    acc[(half, j)] = psum.tile([P, NH], F32, tag="bank", name="acc%d%d" % (half, j))
                tok = slice(P * g, P * (g + 1))
                nc.tensor.matmul_mx(
                    out=acc[(half, j)][:],
                    lhsT=h_codes[:, j, tok].bitcast(FP8X4),
                    lhsT_scale=h_scales[:, j, tok],
                    rhs=w_codes[:, g, cols].bitcast(FP8X4),
                    rhs_scale=w_scales[:, g, cols],
                    start=(g == 0),
                    stop=(g == PASSES - 1),
                )

        haT_ps = psum.tile([P, 4, P], BF16, tag="bank", name="haT_ps")
        for j in range(4):
            nc.tensor.transpose(haT_ps[:, j, :], ha_sb[:, j, :], ident_b[:])
        nc.scalar.copy(out=haT[:], in_=haT_ps[:])

        def lora(l):
            half, j = l // 4, l % 4
            if (half, j) in PE_TILES:
                return
            cols = slice(NH * half, NH * (half + 1))
            lp = psum.tile([P, NH], F32, tag="bank", name="lora_ps")
            nc.tensor.matmul(lp[:], lhsT=haT[:, j, :], rhs=b_sb[:, cols], start=True, stop=True)
            nc.scalar.copy(out=lora_sb[:, j, cols], in_=lp[:])

        hg = []
        late = []

        def quant_h(j, parts=((0, 4 * P), (4 * P, 5 * P))):
            for c0, c1 in parts:
                nc.vector.quantize_mx(
                    out=h_codes[:, j, c0:c1].bitcast(FP8X4),
                    scales=h_scales[:, j, c0:c1],
                    in_=hg[j][:, 4 * c0 : 4 * c1],
                )

        for j in range(4):
            t = keep.tile([P, 4 * PASSES * P], BF16, name="hg%d" % j, align_bytes=64)
            hg.append(t)
            t32 = t[:].bitcast(F32).rearrange("p (g r u) -> p g r u", r=P, u=2)
            words = h_sb[j][:].bitcast(F32)
            for n, (g0, g1) in enumerate(((0, 2), (2, 4), (4, 5))):
                xt = psum.tile([P, g1 - g0, 2, P], F32, tag="bank", name="xt")
                for g in range(g0, g1):
                    for u in range(2):
                        nc.tensor.transpose(
                            xt[:, g - g0, u, :], words[:, 256 * g + u : 256 * (g + 1) : 2], ident_f[:]
                        )
                dst = t32[:, g0:g1, :, :]
                src = xt[:].rearrange("p g u r -> p g r u")
                if n == 2 and j == 3:
                    late.append((dst, src))
                elif n > 0:
                    nc.scalar.copy(out=dst, in_=src)
                else:
                    nc.vector.tensor_copy(out=dst, in_=src)
            if j > 0:
                quant_h(j - 1)
            lora(2 * j)
            lora(2 * j + 1)

        interleave(0)
        nc.scalar.copy(out=late[0][0], in_=late[0][1])
        interleave(1)
        quant_h(3, ((0, 4 * P),))
        quant(0)
        mm(0)
        for i in range(2, 8):
            interleave(i)
            quant(i - 1)
            mm(i - 1)
            if i == 4:
                quant_h(3, ((4 * P, 5 * P),))
        quant(7)
        mm(7)
        interleave(8)
        interleave(9)
        quant(8)
        mm(8)
        quant(9)
        mm(9, (2, 3, 0, 1))

        def tile_of(half, j):
            c0 = D * j + NH * half
            return out_sb[:, c0 : c0 + NH], lora_sb[:, j, NH * half : NH * (half + 1)]

        def store0(half, j):
            o, lo = tile_of(half, j)
            nc.sync.dma_start(out=out0_v[:, j, NH * half : NH * (half + 1)], in_=o)

        def pool_add(half, j):
            o, lo = tile_of(half, j)
            mx = keep.tile([P, NH], F32, name="mx%d%d" % (half, j))
            nc.scalar.copy(out=mx[:], in_=acc[(half, j)][:])
            nc.gpsimd.tensor_tensor(out=o, in0=mx[:], in1=lo, op=ALU.add)

        def add(half, j):
            o, lo = tile_of(half, j)
            nc.vector.tensor_tensor(out=o, in0=acc[(half, j)][:], in1=lo, op=ALU.add)
            store0(half, j)

        def red(half, j, n):
            c0 = D * j + NH * half
            nc.vector.tensor_reduce(
                out=out_sb[:, 4 * D + n : 4 * D + n + 1], in_=out_sb[:, c0 : c0 + NH], axis=AX.X, op=ALU.max,
                apply_absolute_value=True,
            )

        both = {}
        mxs = {}

        def pe_open(half, j):
            both[(half, j)] = psum.tile([P, NH], F32, tag="bank", name="both%d%d" % (half, j))
            nc.tensor.matmul(
                both[(half, j)][:], lhsT=haT[:, j, :], rhs=b_sb[:, NH * half : NH * (half + 1)], start=True, stop=False
            )

        def pe_in(half, j):
            mxs[(half, j)] = keep.tile([P, NH], F32, name="mx%d%d" % (half, j))
            nc.scalar.copy(out=mxs[(half, j)][:], in_=acc[(half, j)][:])
            nc.tensor.matmul(both[(half, j)][:], lhsT=ident_f[:], rhs=mxs[(half, j)][:], start=False, stop=True)

        def pe_out(half, j):
            o, lo = tile_of(half, j)
            nc.scalar.copy(out=o, in_=both[(half, j)][:])

        pool_add(0, 1)
        pool_add(0, 3)
        add(0, 0)
        add(0, 2)
        red(0, 0, 0)
        red(0, 2, 1)
        pe_open(1, 2)
        pe_open(1, 3)
        pe_in(1, 2)
        pe_in(1, 3)
        add(1, 0)
        pool_add(1, 1)
        pe_out(1, 2)
        pe_out(1, 3)
        idle_ps = psum.tile([P, NH], F32, tag="bank", name="idle_ps")
        for n in range(N_IDLE):
            nc.tensor.matmul(idle_ps[:], lhsT=ident_b[:], rhs=idle_rhs[:], start=True, stop=True)
        store0(0, 1)
        red(0, 1, 2)
        red(1, 0, 3)
        store0(0, 3)
        red(0, 3, 4)
        store0(1, 2)
        red(1, 2, 5)
        store0(1, 1)
        red(1, 1, 6)
        store0(1, 3)
        nc.vector.tensor_reduce(
            out=stat[:, 0:1], in_=out_sb[:, 3 * D + NH : 4 * D + 7], axis=AX.X, op=ALU.max, apply_absolute_value=True
        )

        am_ps = psum.tile([P, P], F32, tag="bank", name="am_ps")
        nc.tensor.transpose(am_ps[:], stat[:, 0:1].to_broadcast([P, P]), ident_f[:])
        am_sb = keep.tile([P, P], F32, name="am_sb")
        nc.vector.tensor_scalar(
            out=am_sb[:], in0=am_ps[:], scalar1=1.0 / 448.0, scalar2=None, op0=ALU.mult, op1=ALU.max,
            accum_out=stat[:, 1:2],
        )
        nc.vector.reciprocal(out=stat[:, 3:4], in_=stat[:, 1:2])
        r = stat[:, 3:4]

        o_flat = out_sb
        f8 = [keep.tile([P, D], FP8, name="f8_%d" % j) for j in range(4)]

        def v_cast(a, b):
            j = a // D
            nc.vector.tensor_scalar(
                out=f8[j][:, a - D * j : b - D * j], in0=o_flat[:, a:b], scalar1=r, scalar2=None, op0=ALU.mult,
                saturate=False,
            )

        def s_cast(a, b):
            j = a // D
            nc.scalar.activation(
                out=f8[j][:, a - D * j : b - D * j], in_=o_flat[:, a:b], func=ACT.Identity, scale=r,
                bias=zero[:, 0:1], saturate=False,
            )

        def store(j):
            nc.sync.dma_start(out=out1_v[:, j, :], in_=f8[j][:].bitcast(U8))

        s_cast(3 * D, 4 * D)
        v_cast(0, D)
        store(0)
        v_cast(D, 2 * D)
        store(1)
        store(3)
        s_cast(S_FROM, 3 * D)
        v_cast(2 * D, S_FROM)
        store(2)
